import numpy as np
import ml_dtypes


def mxq(x, axis, fmt="e4m3"):
    dtype, down = {"e4m3": (ml_dtypes.float8_e4m3fn, 7), "e5m2": (ml_dtypes.float8_e5m2, 14)}[fmt]
    v = np.moveaxis(np.asarray(x, np.float32).astype(ml_dtypes.bfloat16).astype(np.float64), axis, -1)
    blocks = v.reshape(v.shape[:-1] + (-1, 32))
    amax = np.abs(blocks).max(-1, keepdims=True)
    byte = np.maximum(np.where(amax > 0, np.frexp(amax)[1] - 1 + 127, 0) - down, 1)
    scale = np.exp2(byte - 127.0)
    codes = (blocks / scale).astype(np.float32).astype(dtype).astype(np.float64)
    return np.moveaxis((codes * scale).reshape(v.shape), -1, axis)


WIDE = False


def mx_kscale(k):
    if not WIDE:
        return np.ones(k)
    levels = np.array([10, -10, 5, -5, 0])
    a = np.random.permutation(np.resize(levels, k // 512 * 4)).reshape(k // 512, 4)
    idx = np.arange(k)
    return np.exp2(a[idx // 512, idx % 128 // 32])


BF16 = ml_dtypes.bfloat16


def bf(x):
    return np.asarray(x, np.float32).astype(BF16)


def f64(x):
    return np.asarray(x).astype(np.float64)


B, S, H, O, W = 8, 2048, 512, 128, 8


def setup_inputs():
    s = mx_kscale(H)
    return {"hidden_states": bf(np.random.standard_normal((B, S, H)) * s),
            "gate_proj": bf(np.random.standard_normal((O, H)) / np.sqrt(H) / s[None, :]),
            "world_size": W}


def reference(hidden_states, gate_proj, world_size):
    h = gate_proj.shape[1]
    view = f64(hidden_states).reshape(-1, h)
    mm = mxq(view, 1, "e4m3") @ mxq(f64(gate_proj), 1, "e4m3").T
    n, o = mm.shape
    out = mm.reshape(world_size, n // world_size, o).sum(axis=0)
    return out

@@ -1,0 +1,164 @@
+from contextlib import ExitStack
+
+import concourse.mybir as mybir
+from concourse.masks import make_identity
+
+F32 = mybir.dt.float32
+BF16 = mybir.dt.bfloat16
+U32 = mybir.dt.uint32
+U8 = mybir.dt.uint8
+FP8X4 = mybir.dt.float8_e4m3fn_x4
+
+P = 128
+PACK = 4
+HALVES = 2
+
+CHUNKS = 8
+ROWS = 2048
+K = 512
+WIDTH = 128
+
+ROWS_PER_PARTITION = ROWS // P
+UNIT_BLOCKS = 4
+STRIPS = ROWS_PER_PARTITION // UNIT_BLOCKS
+UNITS = STRIPS * CHUNKS
+BANK_BLOCKS = 2
+UNIT_BANKS = UNIT_BLOCKS // BANK_BLOCKS
+BANK_WORDS = BANK_BLOCKS * HALVES * P
+RUN_UNITS = 2
+RUNS = UNITS // RUN_UNITS
+VECTOR_EVERY = 4
+
+FLOPS = 2 * CHUNKS * ROWS * K * WIDTH
+
+
+def tile_testmmrsmodel_t_kernel(tc, hidden_states, gate_proj, world_size, out):
+    nc = tc.nc
+    assert world_size == CHUNKS
+    assert tuple(hidden_states.shape) == (CHUNKS, ROWS, K)
+    assert tuple(gate_proj.shape) == (WIDTH, K)
+
+    x_dram = hidden_states.rearrange("r (p i) k -> p r (i k)", i=ROWS_PER_PARTITION)
+    out_dram = out.rearrange("(p i) o -> p (i o)", i=ROWS_PER_PARTITION)
+
+    with ExitStack() as stack:
+        const = stack.enter_context(tc.tile_pool(name="const", bufs=1))
+        x_pool = stack.enter_context(tc.tile_pool(name="x", bufs=UNITS))
+        staged = stack.enter_context(tc.tile_pool(name="staged", bufs=3 * RUN_UNITS))
+        out_pool = stack.enter_context(tc.tile_pool(name="result", bufs=2))
+        flipped = stack.enter_context(tc.psum_pool(name="flipped", bufs=RUN_UNITS * UNIT_BANKS))
+        sums_pool = stack.enter_context(tc.psum_pool(name="sums", bufs=1))
+        stack.enter_context(tc.manual_schedule())
+
+        identity = const.tile([P, P], F32)
+        gate = const.tile([P, K], BF16)
+        gate_grouped = const.tile([P, WIDTH * PACK], BF16, align_bytes=64)
+        gate_codes = const.tile([P, WIDTH], U32, align_bytes=64)
+        gate_scales = const.tile([P, WIDTH], U8, align_bytes=64)
+
+        x_tiles = {}
+        grouped_tiles = {}
+        mx_tiles = {}
+        sums = {}
+
+        def load(unit):
+            strip, chunk = divmod(unit, CHUNKS)
+            x = x_pool.tile([P, UNIT_BLOCKS * K], BF16)
+            first = strip * UNIT_BLOCKS * K
+            nc.sync.dma_start(out=x[:], in_=x_dram[:, chunk, first : first + UNIT_BLOCKS * K])
+            x_tiles[unit] = x
+
+        def transpose_block(bank_part, words):
+            for u in range(HALVES):
+                nc.tensor.transpose(bank_part[:, u, :], words[:, u * P : (u + 1) * P], identity[:])
+
+        def transpose_unit(unit):
+            words = x_tiles[unit][:].bitcast(F32)
+            grouped = staged.tile([P, UNIT_BLOCKS * P * PACK], BF16, align_bytes=64)
+            grouped_words = grouped[:].bitcast(F32)
+            for h in range(UNIT_BANKS):
+                bank = flipped.tile([P, BANK_BLOCKS, HALVES, P], F32)
+                for a in range(BANK_BLOCKS):
+                    first = (h * BANK_BLOCKS + a) * HALVES * P
+                    transpose_block(bank[:, a], words[:, first : first + HALVES * P])
+                src = bank[:].rearrange("p a u j -> p a j u")
+                dst = grouped_words[:, h * BANK_WORDS : (h + 1) * BANK_WORDS].rearrange(
+                    "p (a j u) -> p a j u", a=BANK_BLOCKS, u=HALVES
+                )
+                if (unit * UNIT_BANKS + h) % VECTOR_EVERY == VECTOR_EVERY - 1:
+                    nc.vector.tensor_copy(out=dst, in_=src)
+                else:
+                    nc.scalar.copy(out=dst, in_=src)
+            grouped_tiles[unit] = grouped
+
+        def prepare_gate():
+            bank = flipped.tile([P, BANK_BLOCKS, HALVES, P], F32)
+            transpose_block(bank[:, 0], gate[:].bitcast(F32))
+            nc.vector.tensor_copy(
+                out=gate_grouped[:].bitcast(F32).rearrange("p (j u) -> p j u", u=HALVES),
+                in_=bank[:, 0].rearrange("p u j -> p j u"),
+            )
+            nc.vector.quantize_mx(
+                out=gate_codes[:].bitcast(FP8X4), scales=gate_scales[:], in_=gate_grouped[:]
+            )
+
+        def quantise_unit(unit):
+            codes = staged.tile([P, UNIT_BLOCKS * P], U32, align_bytes=64)
+            scales = staged.tile([P, UNIT_BLOCKS * P], U8, align_bytes=64)
+            nc.vector.quantize_mx(
+                out=codes[:].bitcast(FP8X4), scales=scales[:], in_=grouped_tiles[unit][:]
+            )
+            mx_tiles[unit] = (codes, scales)
+
+        def multiply_unit(unit):
+            strip, chunk = divmod(unit, CHUNKS)
+            codes, scales = mx_tiles[unit]
+            for b in range(UNIT_BLOCKS):
+                if chunk == 0:
+                    sums[b] = sums_pool.tile([P, WIDTH], F32, name="sum%d" % b)
+                rows = slice(b * P, (b + 1) * P)
+                nc.tensor.matmul_mx(
+                    out=sums[b][:],
+                    lhsT=codes[:, rows].bitcast(FP8X4),
+                    lhsT_scale=scales[:, rows],
+                    rhs=gate_codes[:].bitcast(FP8X4),
+                    rhs_scale=gate_scales[:],
+                    start=(chunk == 0),
+                    stop=(chunk == CHUNKS - 1),
+                )
+            if chunk == CHUNKS - 1:
+                store_strip(strip)
+
+        def store_strip(strip):
+            result = out_pool.tile([P, UNIT_BLOCKS, WIDTH], F32)
+            for b in range(UNIT_BLOCKS):
+                if b % 2 == 0:
+                    nc.scalar.copy(out=result[:, b, :], in_=sums[b][:])
+                else:
+                    nc.vector.tensor_copy(out=result[:, b, :], in_=sums[b][:])
+            first = strip * UNIT_BLOCKS * WIDTH
+            nc.sync.dma_start(
+                out=out_dram[:, first : first + UNIT_BLOCKS * WIDTH],
+                in_=result[:].rearrange("p b o -> p (b o)"),
+            )
+
+        def units_of(run):
+            return range(run * RUN_UNITS, (run + 1) * RUN_UNITS)
+
+        nc.scalar.dma_start(out=gate[:], in_=gate_proj)
+        for unit in range(UNITS):
+            load(unit)
+        make_identity(nc, identity[:])
+
+        for t in range(RUNS + 2):
+            if 1 <= t <= RUNS:
+                for unit in units_of(t - 1):
+                    quantise_unit(unit)
+            if t < RUNS:
+                for unit in units_of(t):
+                    transpose_unit(unit)
+            if t == 0:
+                prepare_gate()
+            if t >= 2:
+                for unit in units_of(t - 2):
+                    multiply_unit(unit)

@@ -25,7 +25,8 @@ UNITS = STRIPS * CHUNKS
 BANK_BLOCKS = 2
 UNIT_BANKS = UNIT_BLOCKS // BANK_BLOCKS
 BANK_WORDS = BANK_BLOCKS * HALVES * P
-RUN_UNITS = 2
+FLIPPED_BANKS = 4
+RUN_UNITS = 4
 RUNS = UNITS // RUN_UNITS
 VECTOR_EVERY = 4
 
@@ -44,9 +45,10 @@ def tile_testmmrsmodel_t_kernel(tc, hidden_states, gate_proj, world_size, out):
     with ExitStack() as stack:
         const = stack.enter_context(tc.tile_pool(name="const", bufs=1))
         x_pool = stack.enter_context(tc.tile_pool(name="x", bufs=UNITS))
-        staged = stack.enter_context(tc.tile_pool(name="staged", bufs=3 * RUN_UNITS))
+        grouped_pool = stack.enter_context(tc.tile_pool(name="grouped", bufs=3))
+        mx_pool = stack.enter_context(tc.tile_pool(name="mx", bufs=2 * RUN_UNITS))
         out_pool = stack.enter_context(tc.tile_pool(name="result", bufs=2))
-        flipped = stack.enter_context(tc.psum_pool(name="flipped", bufs=RUN_UNITS * UNIT_BANKS))
+        flipped = stack.enter_context(tc.psum_pool(name="flipped", bufs=FLIPPED_BANKS))
         sums_pool = stack.enter_context(tc.psum_pool(name="sums", bufs=1))
         stack.enter_context(tc.manual_schedule())
 
@@ -74,7 +76,7 @@ def tile_testmmrsmodel_t_kernel(tc, hidden_states, gate_proj, world_size, out):
 
         def transpose_unit(unit):
             words = x_tiles[unit][:].bitcast(F32)
-            grouped = staged.tile([P, UNIT_BLOCKS * P * PACK], BF16, align_bytes=64)
+            grouped = grouped_pool.tile([P, UNIT_BLOCKS * P * PACK], BF16, align_bytes=64)
             grouped_words = grouped[:].bitcast(F32)
             for h in range(UNIT_BANKS):
                 bank = flipped.tile([P, BANK_BLOCKS, HALVES, P], F32)
@@ -103,8 +105,8 @@ def tile_testmmrsmodel_t_kernel(tc, hidden_states, gate_proj, world_size, out):
             )
 
         def quantise_unit(unit):
-            codes = staged.tile([P, UNIT_BLOCKS * P], U32, align_bytes=64)
-            scales = staged.tile([P, UNIT_BLOCKS * P], U8, align_bytes=64)
+            codes = mx_pool.tile([P, UNIT_BLOCKS * P], U32, align_bytes=64)
+            scales = mx_pool.tile([P, UNIT_BLOCKS * P], U8, align_bytes=64)
             nc.vector.quantize_mx(
                 out=codes[:].bitcast(FP8X4), scales=scales[:], in_=grouped_tiles[unit][:]
             )
@@ -150,15 +152,16 @@ def tile_testmmrsmodel_t_kernel(tc, hidden_states, gate_proj, world_size, out):
             load(unit)
         make_identity(nc, identity[:])
 
-        for t in range(RUNS + 2):
-            if 1 <= t <= RUNS:
-                for unit in units_of(t - 1):
-                    quantise_unit(unit)
+        for t in range(RUNS + 1):
             if t < RUNS:
                 for unit in units_of(t):
+                    if unit >= 1:
+                        quantise_unit(unit - 1)
                     transpose_unit(unit)
+            else:
+                quantise_unit(UNITS - 1)
             if t == 0:
                 prepare_gate()
-            if t >= 2:
-                for unit in units_of(t - 2):
+            else:
+                for unit in units_of(t - 1):
                     multiply_unit(unit)

@@ -25,10 +25,12 @@ UNITS = STRIPS * CHUNKS
 BANK_BLOCKS = 2
 UNIT_BANKS = UNIT_BLOCKS // BANK_BLOCKS
 BANK_WORDS = BANK_BLOCKS * HALVES * P
-FLIPPED_BANKS = 4
-RUN_UNITS = 4
+RUN_UNITS = 2
 RUNS = UNITS // RUN_UNITS
 VECTOR_EVERY = 4
+
+UNITS_BEFORE_FIRST_PASS = 3 * RUN_UNITS
+FIRST_FILLERS = 4
 
 FLOPS = 2 * CHUNKS * ROWS * K * WIDTH
 
@@ -45,10 +47,9 @@ def tile_testmmrsmodel_t_kernel(tc, hidden_states, gate_proj, world_size, out):
     with ExitStack() as stack:
         const = stack.enter_context(tc.tile_pool(name="const", bufs=1))
         x_pool = stack.enter_context(tc.tile_pool(name="x", bufs=UNITS))
-        grouped_pool = stack.enter_context(tc.tile_pool(name="grouped", bufs=3))
-        mx_pool = stack.enter_context(tc.tile_pool(name="mx", bufs=2 * RUN_UNITS))
+        staged = stack.enter_context(tc.tile_pool(name="staged", bufs=3 * RUN_UNITS))
         out_pool = stack.enter_context(tc.tile_pool(name="result", bufs=2))
-        flipped = stack.enter_context(tc.psum_pool(name="flipped", bufs=FLIPPED_BANKS))
+        flipped = stack.enter_context(tc.psum_pool(name="flipped", bufs=RUN_UNITS * UNIT_BANKS))
         sums_pool = stack.enter_context(tc.psum_pool(name="sums", bufs=1))
         stack.enter_context(tc.manual_schedule())
 
@@ -63,6 +64,17 @@ def tile_testmmrsmodel_t_kernel(tc, hidden_states, gate_proj, world_size, out):
         mx_tiles = {}
         sums = {}
 
+        idle_banks = [sums_pool.tile([P, K], F32, name="sum%d" % b) for b in range(UNIT_BLOCKS)]
+
+        def filler(count):
+            nc.tensor.matmul(
+                out=idle_banks[count % UNIT_BLOCKS][:],
+                lhsT=gate[:, 0:P],
+                rhs=gate[:],
+                start=True,
+                stop=True,
+            )
+
         def load(unit):
             strip, chunk = divmod(unit, CHUNKS)
             x = x_pool.tile([P, UNIT_BLOCKS * K], BF16)
@@ -76,7 +88,7 @@ def tile_testmmrsmodel_t_kernel(tc, hidden_states, gate_proj, world_size, out):
 
         def transpose_unit(unit):
             words = x_tiles[unit][:].bitcast(F32)
-            grouped = grouped_pool.tile([P, UNIT_BLOCKS * P * PACK], BF16, align_bytes=64)
+            grouped = staged.tile([P, UNIT_BLOCKS * P * PACK], BF16, align_bytes=64)
             grouped_words = grouped[:].bitcast(F32)
             for h in range(UNIT_BANKS):
                 bank = flipped.tile([P, BANK_BLOCKS, HALVES, P], F32)
@@ -92,6 +104,8 @@ def tile_testmmrsmodel_t_kernel(tc, hidden_states, gate_proj, world_size, out):
                 else:
                     nc.scalar.copy(out=dst, in_=src)
             grouped_tiles[unit] = grouped
+            if unit < UNITS_BEFORE_FIRST_PASS:
+                filler(unit)
 
         def prepare_gate():
             bank = flipped.tile([P, BANK_BLOCKS, HALVES, P], F32)
@@ -105,8 +119,8 @@ def tile_testmmrsmodel_t_kernel(tc, hidden_states, gate_proj, world_size, out):
             )
 
         def quantise_unit(unit):
-            codes = mx_pool.tile([P, UNIT_BLOCKS * P], U32, align_bytes=64)
-            scales = mx_pool.tile([P, UNIT_BLOCKS * P], U8, align_bytes=64)
+            codes = staged.tile([P, UNIT_BLOCKS * P], U32, align_bytes=64)
+            scales = staged.tile([P, UNIT_BLOCKS * P], U8, align_bytes=64)
             nc.vector.quantize_mx(
                 out=codes[:].bitcast(FP8X4), scales=scales[:], in_=grouped_tiles[unit][:]
             )
@@ -151,17 +165,18 @@ def tile_testmmrsmodel_t_kernel(tc, hidden_states, gate_proj, world_size, out):
         for unit in range(UNITS):
             load(unit)
         make_identity(nc, identity[:])
+        for count in range(FIRST_FILLERS):
+            filler(count)
 
-        for t in range(RUNS + 1):
+        for t in range(RUNS + 2):
+            if 1 <= t <= RUNS:
+                for unit in units_of(t - 1):
+                    quantise_unit(unit)
             if t < RUNS:
                 for unit in units_of(t):
-                    if unit >= 1:
-                        quantise_unit(unit - 1)
                     transpose_unit(unit)
-            else:
-                quantise_unit(UNITS - 1)
             if t == 0:
                 prepare_gate()
-            else:
-                for unit in units_of(t - 1):
+            if t >= 2:
+                for unit in units_of(t - 2):
                     multiply_unit(unit)

from contextlib import ExitStack

import concourse.mybir as mybir
from concourse.masks import make_identity

F32 = mybir.dt.float32
BF16 = mybir.dt.bfloat16
U32 = mybir.dt.uint32
U8 = mybir.dt.uint8
FP8X4 = mybir.dt.float8_e4m3fn_x4

P = 128
PACK = 4
HALVES = 2

CHUNKS = 8
ROWS = 2048
K = 512
WIDTH = 128

ROWS_PER_PARTITION = ROWS // P
UNIT_BLOCKS = 4
STRIPS = ROWS_PER_PARTITION // UNIT_BLOCKS
UNITS = STRIPS * CHUNKS
BANK_BLOCKS = 2
UNIT_BANKS = UNIT_BLOCKS // BANK_BLOCKS
BANK_WORDS = BANK_BLOCKS * HALVES * P
RUN_UNITS = 2
RUNS = UNITS // RUN_UNITS
VECTOR_EVERY = 4

UNITS_BEFORE_FIRST_PASS = 3 * RUN_UNITS
FIRST_FILLERS = 4

FLOPS = 2 * CHUNKS * ROWS * K * WIDTH


def tile_testmmrsmodel_t_kernel(tc, hidden_states, gate_proj, world_size, out):
    nc = tc.nc
    assert world_size == CHUNKS
    assert tuple(hidden_states.shape) == (CHUNKS, ROWS, K)
    assert tuple(gate_proj.shape) == (WIDTH, K)

    x_dram = hidden_states.rearrange("r (p i) k -> p r (i k)", i=ROWS_PER_PARTITION)
    out_dram = out.rearrange("(p i) o -> p (i o)", i=ROWS_PER_PARTITION)

    with ExitStack() as stack:
        const = stack.enter_context(tc.tile_pool(name="const", bufs=1))
        x_pool = stack.enter_context(tc.tile_pool(name="x", bufs=UNITS))
        staged = stack.enter_context(tc.tile_pool(name="staged", bufs=3 * RUN_UNITS))
        out_pool = stack.enter_context(tc.tile_pool(name="result", bufs=2))
        flipped = stack.enter_context(tc.psum_pool(name="flipped", bufs=RUN_UNITS * UNIT_BANKS))
        sums_pool = stack.enter_context(tc.psum_pool(name="sums", bufs=1))
        stack.enter_context(tc.manual_schedule())

        identity = const.tile([P, P], F32)
        gate = const.tile([P, K], BF16)
        gate_grouped = const.tile([P, WIDTH * PACK], BF16, align_bytes=64)
        gate_codes = const.tile([P, WIDTH], U32, align_bytes=64)
        gate_scales = const.tile([P, WIDTH], U8, align_bytes=64)

        x_tiles = {}
        grouped_tiles = {}
        mx_tiles = {}
        sums = {}

        idle_banks = [sums_pool.tile([P, K], F32, name="sum%d" % b) for b in range(UNIT_BLOCKS)]

        def filler(count):
            nc.tensor.matmul(
                out=idle_banks[count % UNIT_BLOCKS][:],
                lhsT=gate[:, 0:P],
                rhs=gate[:],
                start=True,
                stop=True,
            )

        def load(unit):
            strip, chunk = divmod(unit, CHUNKS)
            x = x_pool.tile([P, UNIT_BLOCKS * K], BF16)
            first = strip * UNIT_BLOCKS * K
            nc.sync.dma_start(out=x[:], in_=x_dram[:, chunk, first : first + UNIT_BLOCKS * K])
            x_tiles[unit] = x

        def transpose_block(bank_part, words):
            for u in range(HALVES):
                nc.tensor.transpose(bank_part[:, u, :], words[:, u * P : (u + 1) * P], identity[:])

        def transpose_unit(unit):
            words = x_tiles[unit][:].bitcast(F32)
            grouped = staged.tile([P, UNIT_BLOCKS * P * PACK], BF16, align_bytes=64)
            grouped_words = grouped[:].bitcast(F32)
            for h in range(UNIT_BANKS):
                bank = flipped.tile([P, BANK_BLOCKS, HALVES, P], F32)
                for a in range(BANK_BLOCKS):
                    first = (h * BANK_BLOCKS + a) * HALVES * P
                    transpose_block(bank[:, a], words[:, first : first + HALVES * P])
                src = bank[:].rearrange("p a u j -> p a j u")
                dst = grouped_words[:, h * BANK_WORDS : (h + 1) * BANK_WORDS].rearrange(
                    "p (a j u) -> p a j u", a=BANK_BLOCKS, u=HALVES
                )
                if (unit * UNIT_BANKS + h) % VECTOR_EVERY == VECTOR_EVERY - 1:
                    nc.vector.tensor_copy(out=dst, in_=src)
                else:
                    nc.scalar.copy(out=dst, in_=src)
            grouped_tiles[unit] = grouped
            if unit < UNITS_BEFORE_FIRST_PASS:
                filler(unit)

        def prepare_gate():
            bank = flipped.tile([P, BANK_BLOCKS, HALVES, P], F32)
            transpose_block(bank[:, 0], gate[:].bitcast(F32))
            nc.vector.tensor_copy(
                out=gate_grouped[:].bitcast(F32).rearrange("p (j u) -> p j u", u=HALVES),
                in_=bank[:, 0].rearrange("p u j -> p j u"),
            )
            nc.vector.quantize_mx(
                out=gate_codes[:].bitcast(FP8X4), scales=gate_scales[:], in_=gate_grouped[:]
            )

        def quantise_unit(unit):
            codes = staged.tile([P, UNIT_BLOCKS * P], U32, align_bytes=64)
            scales = staged.tile([P, UNIT_BLOCKS * P], U8, align_bytes=64)
            nc.vector.quantize_mx(
                out=codes[:].bitcast(FP8X4), scales=scales[:], in_=grouped_tiles[unit][:]
            )
            mx_tiles[unit] = (codes, scales)

        def multiply_unit(unit):
            strip, chunk = divmod(unit, CHUNKS)
            codes, scales = mx_tiles[unit]
            for b in range(UNIT_BLOCKS):
                if chunk == 0:
                    sums[b] = sums_pool.tile([P, WIDTH], F32, name="sum%d" % b)
                rows = slice(b * P, (b + 1) * P)
                nc.tensor.matmul_mx(
                    out=sums[b][:],
                    lhsT=codes[:, rows].bitcast(FP8X4),
                    lhsT_scale=scales[:, rows],
                    rhs=gate_codes[:].bitcast(FP8X4),
                    rhs_scale=gate_scales[:],
                    start=(chunk == 0),
                    stop=(chunk == CHUNKS - 1),
                )
            if chunk == CHUNKS - 1:
                store_strip(strip)

        def store_strip(strip):
            result = out_pool.tile([P, UNIT_BLOCKS, WIDTH], F32)
            for b in range(UNIT_BLOCKS):
                if b % 2 == 0:
                    nc.scalar.copy(out=result[:, b, :], in_=sums[b][:])
                else:
                    nc.vector.tensor_copy(out=result[:, b, :], in_=sums[b][:])
            first = strip * UNIT_BLOCKS * WIDTH
            nc.sync.dma_start(
                out=out_dram[:, first : first + UNIT_BLOCKS * WIDTH],
                in_=result[:].rearrange("p b o -> p (b o)"),
            )

        def units_of(run):
            return range(run * RUN_UNITS, (run + 1) * RUN_UNITS)

        nc.scalar.dma_start(out=gate[:], in_=gate_proj)
        for unit in range(UNITS):
            load(unit)
        make_identity(nc, identity[:])
        for count in range(FIRST_FILLERS):
            filler(count)

        for t in range(RUNS + 2):
            if 1 <= t <= RUNS:
                for unit in units_of(t - 1):
                    quantise_unit(unit)
            if t < RUNS:
                for unit in units_of(t):
                    transpose_unit(unit)
            if t == 0:
                prepare_gate()
            if t >= 2:
                for unit in units_of(t - 2):
                    multiply_unit(unit)
